import numpy as np
import ml_dtypes


def mxq(x, axis, fmt="e4m3"):
    dtype, down = {"e4m3": (ml_dtypes.float8_e4m3fn, 7), "e5m2": (ml_dtypes.float8_e5m2, 14)}[fmt]
    v = np.moveaxis(np.asarray(x, np.float32).astype(ml_dtypes.bfloat16).astype(np.float64), axis, -1)
    blocks = v.reshape(v.shape[:-1] + (-1, 32))
    amax = np.abs(blocks).max(-1, keepdims=True)
    byte = np.maximum(np.where(amax > 0, np.frexp(amax)[1] - 1 + 127, 0) - down, 1)
    scale = np.exp2(byte - 127.0)
    codes = (blocks / scale).astype(np.float32).astype(dtype).astype(np.float64)
    return np.moveaxis((codes * scale).reshape(v.shape), -1, axis)


WIDE = False


def mx_kscale(k):
    if not WIDE:
        return np.ones(k)
    levels = np.array([10, -10, 5, -5, 0])
    if k % 512:
        return np.exp2(np.random.permutation(np.resize(levels, k // 32))).repeat(32)
    a = np.empty((k // 512, 16))
    for p in range(k // 512):
        a[p, :8] = np.random.permutation(np.resize(levels, 8))
        for g in range(8):
            far = levels[np.abs(levels - a[p, g]) >= 10]
            a[p, g + 8] = far[np.random.randint(len(far))]
    return np.exp2(a.ravel()).repeat(32)


BF16 = ml_dtypes.bfloat16


def bf(x):
    return np.asarray(x, np.float32).astype(BF16)


def f64(x):
    return np.asarray(x).astype(np.float64)


B, CIN, CM, CO, H, WD = 1, 512, 512, 512, 16, 16
RING = [(-1, -1), (-1, 0), (-1, 1), (0, 1), (1, 1), (1, 0), (1, -1), (0, -1)]
NUM_K = 9
KERNEL_ROT = 4
STEP = 2
M = NUM_K * CM


def setup_inputs():
    s = mx_kscale(CIN)
    t = mx_kscale(CM)
    return {"x": bf(np.random.standard_normal((B, CIN, H, WD)) * s[None, :, None, None]),
            "W": bf(np.random.standard_normal((CM, CIN, NUM_K)) / np.sqrt(CIN) / s[None, :, None] * t[:, None, None]),
            "W1": bf(np.random.standard_normal((CO, M)) * 1.4 / np.sqrt(M) / np.tile(t, NUM_K)[None, :])}


def reference(x, W, W1):
    xq = mxq(f64(x), 1, "e4m3")
    Wq = mxq(f64(W), 1, "e4m3")
    z = (Wq.transpose(0, 2, 1).reshape(CM * NUM_K, CIN) @ xq.reshape(B, CIN, H * WD)).reshape(B, CM, NUM_K, H, WD)
    h = np.maximum(z, 0.0)
    hq = mxq(h, 1, "e4m3")
    W1q = mxq(f64(W1).reshape(CO, NUM_K, CM), 2, "e4m3")
    u = (W1q.transpose(1, 0, 2) @ hq.transpose(0, 2, 1, 3, 4).reshape(B, NUM_K, CM, H * WD)).reshape(B, NUM_K, CO, H, WD)
    up = np.pad(u, ((0, 0), (0, 0), (0, 0), (1, 1), (1, 1)))
    rot_out = []
    for rot in range(KERNEL_ROT):
        roff = STEP * rot
        acc = 0.0
        for k in range(NUM_K):
            dy, dx = (0, 0) if k == NUM_K - 1 else RING[(k + roff) % len(RING)]
            acc = acc + up[:, k, :, 1 + dy:1 + dy + H, 1 + dx:1 + dx + WD]
        rot_out.append(acc)
    return np.stack(rot_out, axis=2)

@@ -1,0 +1,245 @@
+from contextlib import ExitStack
+
+import concourse.masks as masks
+import concourse.mybir as mybir
+
+BF16 = mybir.dt.bfloat16
+F32 = mybir.dt.float32
+U32 = mybir.dt.uint32
+U8 = mybir.dt.uint8
+FP8X4 = mybir.dt.float8_e4m3fn_x4
+RELU = mybir.ActivationFunctionType.Relu
+
+P = 128
+PACK = 4
+CH = 512
+TILES = CH // P
+NUM_K = 9
+CENTRE = 8
+SIDE = 16
+PIXELS = SIDE * SIDE
+ROTATIONS = 4
+RING = [(-1, -1), (-1, 0), (-1, 1), (0, 1), (1, 1), (1, 0), (1, -1), (0, -1)]
+PLANES = 3
+BANKS = 8
+EARLY_GROUPS = 4
+WEIGHTS_LEAD = 3
+HIDDEN_LEAD = 2
+
+FLOPS = 2 * 2 * NUM_K * CH * CH * PIXELS
+
+
+def shift_of(k, r):
+    return (0, 0) if k == CENTRE else RING[(k + 2 * r) % len(RING)]
+
+
+def tile_psr4convf_kernel(tc, x, W, W1, out):
+    nc = tc.nc
+    with ExitStack() as ctx:
+        keep = ctx.enter_context(tc.tile_pool(name="keep", bufs=1))
+        w_in = ctx.enter_context(tc.tile_pool(name="w_in", bufs=TILES))
+        w1_in = ctx.enter_context(tc.tile_pool(name="w1_in", bufs=7))
+        stage = ctx.enter_context(tc.tile_pool(name="stage", bufs=4))
+        psum = ctx.enter_context(tc.psum_pool(name="psum", bufs=BANKS))
+
+        def bank(shape):
+            return psum.tile(shape, F32, tag="bank", name="bank")
+
+        x_rows = keep.tile([P, PACK, PIXELS], BF16)
+        nc.sync.dma_start(
+            out=x_rows[:],
+            in_=x[0].rearrange("(q t) h w -> q t (h w)", t=PACK),
+        )
+        w_dram = W.rearrange("(q t) c k -> t q (c k)", t=PACK)
+        w_rows = []
+        for t in range(TILES):
+            rows = w_in.tile([P, CH * NUM_K], BF16, name="w_rows")
+            nc.sync.dma_start(out=rows[:], in_=w_dram[t])
+            w_rows.append(rows)
+        w1_dram = W1.rearrange("(a q) (k o) -> k q a o", q=P, k=NUM_K)
+        w1_rows = []
+        for k in range(NUM_K):
+            rows = w1_in.tile([P, TILES * CH], BF16, name="w1_rows")
+            nc.sync.dma_start(out=rows[:].rearrange("q (a o) -> q a o", a=TILES), in_=w1_dram[k])
+            w1_rows.append(rows)
+
+        ident = keep.tile([P, P], F32)
+        masks.make_identity(nc, ident[:])
+        padded = (SIDE + 2) * SIDE * PACK
+        h_image = {}
+        for dx in (-1, 0, 1):
+            for slot in range(2):
+                image = keep.tile([P, padded], BF16, align_bytes=64, name="h_image_%d_%d" % (dx + 1, slot))
+                nc.vector.memset(image[:], 0.0)
+                h_image[(dx, slot)] = image
+
+        x_grouped = keep.tile([P, PIXELS, PACK], BF16, align_bytes=64)
+        x_codes = keep.tile([P, PIXELS], U32, align_bytes=64)
+        x_scales = keep.tile([P, PIXELS], U8, align_bytes=64)
+        nc.vector.tensor_copy(out=x_grouped[:], in_=x_rows[:].rearrange("q t n -> q n t"))
+        nc.vector.quantize_mx(
+            out=x_codes[:].bitcast(FP8X4),
+            scales=x_scales[:],
+            in_=x_grouped[:].rearrange("q n t -> q (n t)"),
+        )
+
+        def transpose_and_quantise(first, second, codes, scales):
+            turned = bank([P, 2, 2, P])
+            for a, words in enumerate((first, second)):
+                for u in range(2):
+                    nc.tensor.transpose(turned[:, a, u, :], words[:, u : 2 * P : 2], ident[:])
+            grouped = stage.tile([P, 2 * P * PACK], BF16, align_bytes=64, name="grouped")
+            nc.scalar.copy(
+                out=grouped[:].bitcast(F32).rearrange("q (a c u) -> q a c u", a=2, u=2),
+                in_=turned[:].rearrange("q a u c -> q a c u"),
+            )
+            nc.vector.quantize_mx(out=codes.bitcast(FP8X4), scales=scales, in_=grouped[:])
+
+        w_by_k = [keep.tile([P, NUM_K * CH], BF16, name="w_by_k%d" % t) for t in range(TILES)]
+
+        def take_apart(t, g):
+            ks = slice(g * PLANES, (g + 1) * PLANES)
+            src = w_rows[t][:].rearrange("q (c k) -> q c k", k=NUM_K)[:, :, ks]
+            dst = w_by_k[t][:].rearrange("q (k c) -> q c k", k=NUM_K)[:, :, ks]
+            if g < 2:
+                nc.vector.tensor_copy(out=dst, in_=src)
+            else:
+                nc.scalar.copy(out=dst, in_=src)
+
+        w_codes = keep.tile([P, TILES // 2, NUM_K, 2 * P], U32, align_bytes=64)
+        w_scales = keep.tile([P, TILES // 2, NUM_K, 2 * P], U8, align_bytes=64)
+        w1_codes = keep.tile([P, TILES // 2, NUM_K, 2 * P], U32, align_bytes=64)
+        w1_scales = keep.tile([P, TILES // 2, NUM_K, 2 * P], U8, align_bytes=64)
+        words_of_k = CH // 2
+
+        def weights(k):
+            if k % PLANES == 0:
+                for t in range(TILES):
+                    take_apart(t, k // PLANES)
+            cols = slice(k * words_of_k, (k + 1) * words_of_k)
+            for pair in range(TILES // 2):
+                transpose_and_quantise(
+                    w_by_k[2 * pair][:].bitcast(F32)[:, cols],
+                    w_by_k[2 * pair + 1][:].bitcast(F32)[:, cols],
+                    w_codes[:, pair, k, :],
+                    w_scales[:, pair, k, :],
+                )
+            words = w1_rows[k][:].bitcast(F32)
+            for pair in range(TILES // 2):
+                transpose_and_quantise(
+                    words[:, 2 * pair * words_of_k : (2 * pair + 1) * words_of_k],
+                    words[:, (2 * pair + 1) * words_of_k : (2 * pair + 2) * words_of_k],
+                    w1_codes[:, pair, k, :],
+                    w1_scales[:, pair, k, :],
+                )
+
+        h_codes = keep.tile([P, NUM_K, ROTATIONS // 2, 2 * PIXELS], U32, align_bytes=64)
+        h_scales = keep.tile([P, NUM_K, ROTATIONS // 2, 2 * PIXELS], U8, align_bytes=64)
+
+        def hidden_layer(k):
+            slot = k % 2
+            centred = h_image[(0, slot)]
+            half_pixels = PIXELS // 2
+            for half in range(2):
+                z = bank([P, PACK, half_pixels])
+                pixels = slice(half * half_pixels, (half + 1) * half_pixels)
+                for t in range(TILES):
+                    cols = slice((t % 2) * P, (t % 2 + 1) * P)
+                    nc.tensor.matmul_mx(
+                        out=z[:, t, :],
+                        lhsT=w_codes[:, t // 2, k, cols].bitcast(FP8X4),
+                        lhsT_scale=w_scales[:, t // 2, k, cols],
+                        rhs=x_codes[:, pixels].bitcast(FP8X4),
+                        rhs_scale=x_scales[:, pixels],
+                        start=True,
+                        stop=True,
+                    )
+                begin = (SIDE + half * half_pixels) * PACK
+                nc.scalar.activation(
+                    out=centred[:, begin : begin + half_pixels * PACK].rearrange("q (n t) -> q n t", t=PACK),
+                    in_=z[:].rearrange("q t n -> q n t"),
+                    func=RELU,
+                )
+            shifts = [shift_of(k, r) for r in range(1 if k == CENTRE else ROTATIONS)]
+            for dx in (-1, 1):
+                if any(s[1] == dx for s in shifts):
+                    lo, hi = max(0, -dx), SIDE - max(0, dx)
+                    src = centred[:].rearrange("q (i j t) -> q i j t", j=SIDE, t=PACK)
+                    dst = h_image[(dx, slot)][:].rearrange("q (i j t) -> q i j t", j=SIDE, t=PACK)
+                    nc.vector.tensor_copy(
+                        out=dst[:, 1 : SIDE + 1, lo:hi, :], in_=src[:, 1 : SIDE + 1, lo + dx : hi + dx, :]
+                    )
+            for r, (dy, dx) in enumerate(shifts):
+                begin = (1 + dy) * SIDE * PACK
+                cols = slice((r % 2) * PIXELS, (r % 2 + 1) * PIXELS)
+                nc.vector.quantize_mx(
+                    out=h_codes[:, k, r // 2, cols].bitcast(FP8X4),
+                    scales=h_scales[:, k, r // 2, cols],
+                    in_=h_image[(dx, slot)][:, begin : begin + PIXELS * PACK],
+                )
+
+        def add_position(total, a, k, pair):
+            cols = slice((a % 2) * P, (a % 2 + 1) * P)
+            nc.tensor.matmul_mx(
+                out=total[:],
+                lhsT=w1_codes[:, a // 2, k, cols].bitcast(FP8X4),
+                lhsT_scale=w1_scales[:, a // 2, k, cols],
+                rhs=h_codes[:, k, pair, :].bitcast(FP8X4),
+                rhs_scale=h_scales[:, k, pair, :],
+                start=(k == 0),
+                stop=(k == CENTRE - 1),
+            )
+
+        centre = keep.tile([P, TILES, PIXELS], F32)
+
+        def centre_product():
+            for pair in range(TILES // 2):
+                product = bank([P, 2, PIXELS])
+                for half in range(2):
+                    cols = slice(half * P, (half + 1) * P)
+                    nc.tensor.matmul_mx(
+                        out=product[:, half, :],
+                        lhsT=w1_codes[:, pair, CENTRE, cols].bitcast(FP8X4),
+                        lhsT_scale=w1_scales[:, pair, CENTRE, cols],
+                        rhs=h_codes[:, CENTRE, 0, 0:PIXELS].bitcast(FP8X4),
+                        rhs_scale=h_scales[:, CENTRE, 0, 0:PIXELS],
+                        start=True,
+                        stop=True,
+                    )
+                nc.scalar.copy(out=centre[:, 2 * pair : 2 * pair + 2, :], in_=product[:])
+
+        out_dram = out[0].rearrange("(a q) (s r) h w -> a s q (r h w)", q=P, s=2)
+
+        def store(total, a, pair):
+            result = stage.tile([P, 2 * PIXELS], F32, name="result")
+            nc.vector.tensor_tensor(
+                out=result[:].rearrange("q (r n) -> q r n", r=2),
+                in0=total[:].rearrange("q (r n) -> q r n", r=2),
+                in1=centre[:, a, :].unsqueeze(1).to_broadcast([P, 2, PIXELS]),
+                op=mybir.AluOpType.add,
+            )
+            nc.sync.dma_start(out=out_dram[a, pair], in_=result[:])
+
+        groups = [(a, pair) for pair in range(ROTATIONS // 2) for a in range(TILES)]
+        totals = [bank([P, 2 * PIXELS]) for g in range(EARLY_GROUPS)]
+        for k in range(WEIGHTS_LEAD):
+            weights(k)
+        for k in range(HIDDEN_LEAD):
+            hidden_layer(k)
+        for k in range(NUM_K):
+            if k + WEIGHTS_LEAD < NUM_K:
+                weights(k + WEIGHTS_LEAD)
+            if k + HIDDEN_LEAD < NUM_K:
+                hidden_layer(k + HIDDEN_LEAD)
+            if k == CENTRE:
+                centre_product()
+            else:
+                for g in range(EARLY_GROUPS):
+                    add_position(totals[g], groups[g][0], k, groups[g][1])
+        for g in range(EARLY_GROUPS):
+            store(totals[g], groups[g][0], groups[g][1])
+        for g in range(EARLY_GROUPS, len(groups)):
+            total = bank([P, 2 * PIXELS])
+            for k in range(CENTRE):
+                add_position(total, groups[g][0], k, groups[g][1])
+            store(total, groups[g][0], groups[g][1])

@@ -70,7 +70,7 @@ def tile_psr4convf_kernel(tc, x, W, W1, out):
         for dx in (-1, 0, 1):
             for slot in range(2):
                 image = keep.tile([P, padded], BF16, align_bytes=64, name="h_image_%d_%d" % (dx + 1, slot))
-                nc.vector.memset(image[:], 0.0)
+                nc.gpsimd.memset(image[:].bitcast(F32), 0.0)
                 h_image[(dx, slot)] = image
 
         x_grouped = keep.tile([P, PIXELS, PACK], BF16, align_bytes=64)
@@ -87,7 +87,7 @@ def tile_psr4convf_kernel(tc, x, W, W1, out):
             turned = bank([P, 2, 2, P])
             for a, words in enumerate((first, second)):
                 for u in range(2):
-                    nc.tensor.transpose(turned[:, a, u, :], words[:, u : 2 * P : 2], ident[:])
+                    nc.tensor.transpose(turned[:, a, u, :], words[:, u, :], ident[:])
             grouped = stage.tile([P, 2 * P * PACK], BF16, align_bytes=64, name="grouped")
             nc.scalar.copy(
                 out=grouped[:].bitcast(F32).rearrange("q (a c u) -> q a c u", a=2, u=2),
@@ -99,12 +99,13 @@ def tile_psr4convf_kernel(tc, x, W, W1, out):
 
         def take_apart(t, g):
             ks = slice(g * PLANES, (g + 1) * PLANES)
-            src = w_rows[t][:].rearrange("q (c k) -> q c k", k=NUM_K)[:, :, ks]
-            dst = w_by_k[t][:].rearrange("q (k c) -> q c k", k=NUM_K)[:, :, ks]
+            src = w_rows[t][:].rearrange("p (q u e k) -> p u q e k", u=2, e=2, k=NUM_K)[:, :, :, :, ks]
+            dst = w_by_k[t][:].rearrange("p (k u q e) -> p u q e k", u=2, e=2, k=NUM_K)[:, :, :, :, ks]
             if g < 2:
                 nc.vector.tensor_copy(out=dst, in_=src)
             else:
-                nc.scalar.copy(out=dst, in_=src)
+                for u in range(2):
+                    nc.scalar.copy(out=dst[:, u], in_=src[:, u])
 
         w_codes = keep.tile([P, TILES // 2, NUM_K, 2 * P], U32, align_bytes=64)
         w_scales = keep.tile([P, TILES // 2, NUM_K, 2 * P], U8, align_bytes=64)
@@ -119,16 +120,16 @@ def tile_psr4convf_kernel(tc, x, W, W1, out):
             cols = slice(k * words_of_k, (k + 1) * words_of_k)
             for pair in range(TILES // 2):
                 transpose_and_quantise(
-                    w_by_k[2 * pair][:].bitcast(F32)[:, cols],
-                    w_by_k[2 * pair + 1][:].bitcast(F32)[:, cols],
+                    w_by_k[2 * pair][:].bitcast(F32)[:, cols].rearrange("p (u q) -> p u q", u=2),
+                    w_by_k[2 * pair + 1][:].bitcast(F32)[:, cols].rearrange("p (u q) -> p u q", u=2),
                     w_codes[:, pair, k, :],
                     w_scales[:, pair, k, :],
                 )
-            words = w1_rows[k][:].bitcast(F32)
+            words = w1_rows[k][:].bitcast(F32).rearrange("p (a q u) -> p a u q", a=TILES, u=2)
             for pair in range(TILES // 2):
                 transpose_and_quantise(
-                    words[:, 2 * pair * words_of_k : (2 * pair + 1) * words_of_k],
-                    words[:, (2 * pair + 1) * words_of_k : (2 * pair + 2) * words_of_k],
+                    words[:, 2 * pair],
+                    words[:, 2 * pair + 1],
                     w1_codes[:, pair, k, :],
                     w1_scales[:, pair, k, :],
                 )

@@ -9,6 +9,7 @@ U32 = mybir.dt.uint32
 U8 = mybir.dt.uint8
 FP8X4 = mybir.dt.float8_e4m3fn_x4
 RELU = mybir.ActivationFunctionType.Relu
+ADD = mybir.AluOpType.add
 
 P = 128
 PACK = 4
@@ -22,9 +23,12 @@ ROTATIONS = 4
 RING = [(-1, -1), (-1, 0), (-1, 1), (0, 1), (1, 1), (1, 0), (1, -1), (0, -1)]
 PLANES = 3
 BANKS = 8
-EARLY_GROUPS = 4
-WEIGHTS_LEAD = 3
-HIDDEN_LEAD = 2
+ORDER = [8, 6, 7, 0, 1, 2, 3, 4, 5]
+FIRST_PART = 5
+BEHIND = 2
+WEIGHTS_LEAD = 4
+STEP_1_LEAD = 3
+H_LEAD = 2
 
 FLOPS = 2 * 2 * NUM_K * CH * CH * PIXELS
 
@@ -37,31 +41,14 @@ def tile_psr4convf_kernel(tc, x, W, W1, out):
     nc = tc.nc
     with ExitStack() as ctx:
         keep = ctx.enter_context(tc.tile_pool(name="keep", bufs=1))
-        w_in = ctx.enter_context(tc.tile_pool(name="w_in", bufs=TILES))
-        w1_in = ctx.enter_context(tc.tile_pool(name="w1_in", bufs=7))
-        stage = ctx.enter_context(tc.tile_pool(name="stage", bufs=4))
+        w_in = ctx.enter_context(tc.tile_pool(name="w_in", bufs=3))
+        w1_in = ctx.enter_context(tc.tile_pool(name="w1_in", bufs=5))
+        stage = ctx.enter_context(tc.tile_pool(name="stage", bufs=8))
+        results = ctx.enter_context(tc.tile_pool(name="results", bufs=6))
         psum = ctx.enter_context(tc.psum_pool(name="psum", bufs=BANKS))
 
         def bank(shape):
             return psum.tile(shape, F32, tag="bank", name="bank")
-
-        x_rows = keep.tile([P, PACK, PIXELS], BF16)
-        nc.sync.dma_start(
-            out=x_rows[:],
-            in_=x[0].rearrange("(q t) h w -> q t (h w)", t=PACK),
-        )
-        w_dram = W.rearrange("(q t) c k -> t q (c k)", t=PACK)
-        w_rows = []
-        for t in range(TILES):
-            rows = w_in.tile([P, CH * NUM_K], BF16, name="w_rows")
-            nc.sync.dma_start(out=rows[:], in_=w_dram[t])
-            w_rows.append(rows)
-        w1_dram = W1.rearrange("(a q) (k o) -> k q a o", q=P, k=NUM_K)
-        w1_rows = []
-        for k in range(NUM_K):
-            rows = w1_in.tile([P, TILES * CH], BF16, name="w1_rows")
-            nc.sync.dma_start(out=rows[:].rearrange("q (a o) -> q a o", a=TILES), in_=w1_dram[k])
-            w1_rows.append(rows)
 
         ident = keep.tile([P, P], F32)
         masks.make_identity(nc, ident[:])
@@ -73,73 +60,95 @@ def tile_psr4convf_kernel(tc, x, W, W1, out):
                 nc.gpsimd.memset(image[:].bitcast(F32), 0.0)
                 h_image[(dx, slot)] = image
 
+        x_rows = keep.tile([P, PACK, PIXELS], BF16)
+        nc.sync.dma_start(out=x_rows[:], in_=x[0].rearrange("(q t) h w -> q t (h w)", t=PACK))
+        w_dram = W.rearrange("(q t) c k -> t q (c k)", t=PACK)
+        w_rows = []
+        for t in range(TILES):
+            rows = w_in.tile([P, CH * NUM_K], BF16, name="w_rows")
+            nc.sync.dma_start(out=rows[:], in_=w_dram[t])
+            w_rows.append(rows)
+        w1_dram = W1.rearrange("(a q) (k o) -> k q a o", q=P, k=NUM_K)
+        w1_rows = {}
+        for k in ORDER:
+            rows = w1_in.tile([P, TILES * CH], BF16, name="w1_rows")
+            nc.sync.dma_start(out=rows[:].rearrange("q (a o) -> q a o", a=TILES), in_=w1_dram[k])
+            w1_rows[k] = rows
+
         x_grouped = keep.tile([P, PIXELS, PACK], BF16, align_bytes=64)
         x_codes = keep.tile([P, PIXELS], U32, align_bytes=64)
         x_scales = keep.tile([P, PIXELS], U8, align_bytes=64)
-        nc.vector.tensor_copy(out=x_grouped[:], in_=x_rows[:].rearrange("q t n -> q n t"))
-        nc.vector.quantize_mx(
-            out=x_codes[:].bitcast(FP8X4),
-            scales=x_scales[:],
-            in_=x_grouped[:].rearrange("q n t -> q (n t)"),
-        )
 
-        def transpose_and_quantise(first, second, codes, scales):
-            turned = bank([P, 2, 2, P])
-            for a, words in enumerate((first, second)):
-                for u in range(2):
-                    nc.tensor.transpose(turned[:, a, u, :], words[:, u, :], ident[:])
-            grouped = stage.tile([P, 2 * P * PACK], BF16, align_bytes=64, name="grouped")
-            nc.scalar.copy(
-                out=grouped[:].bitcast(F32).rearrange("q (a c u) -> q a c u", a=2, u=2),
-                in_=turned[:].rearrange("q a u c -> q a c u"),
+        def prepare_x():
+            nc.vector.tensor_copy(out=x_grouped[:], in_=x_rows[:].rearrange("q t n -> q n t"))
+            nc.vector.quantize_mx(
+                out=x_codes[:].bitcast(FP8X4),
+                scales=x_scales[:],
+                in_=x_grouped[:].rearrange("q n t -> q (n t)"),
             )
-            nc.vector.quantize_mx(out=codes.bitcast(FP8X4), scales=scales, in_=grouped[:])
+
+        def transpose(blocks):
+            n = len(blocks)
+            turned = bank([P, n, 2, P])
+            for b, halves in enumerate(blocks):
+                for u in range(2):
+                    nc.tensor.transpose(turned[:, b, u, :], halves[u], ident[:])
+            grouped = stage.tile([P, n * P * PACK], BF16, align_bytes=64, name="grouped")
+            nc.scalar.copy(
+                out=grouped[:].bitcast(F32).rearrange("q (b c u) -> q b c u", b=n, u=2),
+                in_=turned[:].rearrange("q b u c -> q b c u"),
+            )
+            return grouped
 
         w_by_k = [keep.tile([P, NUM_K * CH], BF16, name="w_by_k%d" % t) for t in range(TILES)]
 
         def take_apart(t, g):
-            ks = slice(g * PLANES, (g + 1) * PLANES)
+            first = min(ORDER[g * PLANES : (g + 1) * PLANES])
+            ks = slice(first, first + PLANES)
             src = w_rows[t][:].rearrange("p (q u e k) -> p u q e k", u=2, e=2, k=NUM_K)[:, :, :, :, ks]
             dst = w_by_k[t][:].rearrange("p (k u q e) -> p u q e k", u=2, e=2, k=NUM_K)[:, :, :, :, ks]
-            if g < 2:
-                nc.vector.tensor_copy(out=dst, in_=src)
-            else:
+            if t == 0 and g == 2:
                 for u in range(2):
                     nc.scalar.copy(out=dst[:, u], in_=src[:, u])
+            else:
+                nc.vector.tensor_copy(out=dst, in_=src)
 
         w_codes = keep.tile([P, TILES // 2, NUM_K, 2 * P], U32, align_bytes=64)
         w_scales = keep.tile([P, TILES // 2, NUM_K, 2 * P], U8, align_bytes=64)
         w1_codes = keep.tile([P, TILES // 2, NUM_K, 2 * P], U32, align_bytes=64)
         w1_scales = keep.tile([P, TILES // 2, NUM_K, 2 * P], U8, align_bytes=64)
-        words_of_k = CH // 2
 
-        def weights(k):
-            if k % PLANES == 0:
-                for t in range(TILES):
-                    take_apart(t, k // PLANES)
-            cols = slice(k * words_of_k, (k + 1) * words_of_k)
-            for pair in range(TILES // 2):
-                transpose_and_quantise(
-                    w_by_k[2 * pair][:].bitcast(F32)[:, cols].rearrange("p (u q) -> p u q", u=2),
-                    w_by_k[2 * pair + 1][:].bitcast(F32)[:, cols].rearrange("p (u q) -> p u q", u=2),
-                    w_codes[:, pair, k, :],
-                    w_scales[:, pair, k, :],
-                )
-            words = w1_rows[k][:].bitcast(F32).rearrange("p (a q u) -> p a u q", a=TILES, u=2)
-            for pair in range(TILES // 2):
-                transpose_and_quantise(
-                    words[:, 2 * pair],
-                    words[:, 2 * pair + 1],
-                    w1_codes[:, pair, k, :],
-                    w1_scales[:, pair, k, :],
-                )
+        pending = []
+
+        def quantise(unit):
+            which, k, pair, grouped = unit
+            codes, scales = (w_codes, w_scales) if which == "w" else (w1_codes, w1_scales)
+            nc.vector.quantize_mx(
+                out=codes[:, pair, k, :].bitcast(FP8X4), scales=scales[:, pair, k, :], in_=grouped[:]
+            )
+
+        def quantise_all(which, k):
+            for unit in list(pending):
+                if unit[0] == which and unit[1] == k:
+                    quantise(unit)
+                    pending.remove(unit)
+
+        def prepare(which, k, pair):
+            tiles = (2 * pair, 2 * pair + 1)
+            if which == "w":
+                words = [w_by_k[t][:].bitcast(F32).rearrange("p (k u q) -> p k u q", k=NUM_K, u=2)[:, k] for t in tiles]
+            else:
+                rows = w1_rows[k][:].bitcast(F32).rearrange("p (a q u) -> p a u q", a=TILES, u=2)
+                words = [rows[:, a] for a in tiles]
+            pending.append((which, k, pair, transpose([[w[:, u, :] for u in range(2)] for w in words])))
+            while len(pending) > BEHIND:
+                quantise(pending.pop(0))
 
         h_codes = keep.tile([P, NUM_K, ROTATIONS // 2, 2 * PIXELS], U32, align_bytes=64)
         h_scales = keep.tile([P, NUM_K, ROTATIONS // 2, 2 * PIXELS], U8, align_bytes=64)
 
-        def hidden_layer(k):
-            slot = k % 2
-            centred = h_image[(0, slot)]
+        def step_1(k):
+            centred = h_image[(0, ORDER.index(k) % 2)]
             half_pixels = PIXELS // 2
             for half in range(2):
                 z = bank([P, PACK, half_pixels])
@@ -161,7 +170,11 @@ def tile_psr4convf_kernel(tc, x, W, W1, out):
                     in_=z[:].rearrange("q t n -> q n t"),
                     func=RELU,
                 )
-            shifts = [shift_of(k, r) for r in range(1 if k == CENTRE else ROTATIONS)]
+
+        def quantise_h(k):
+            slot = ORDER.index(k) % 2
+            centred = h_image[(0, slot)]
+            shifts = [shift_of(k, r) for r in range(2 if k == CENTRE else ROTATIONS)]
             for dx in (-1, 1):
                 if any(s[1] == dx for s in shifts):
                     lo, hi = max(0, -dx), SIDE - max(0, dx)
@@ -179,68 +192,68 @@ def tile_psr4convf_kernel(tc, x, W, W1, out):
                     in_=h_image[(dx, slot)][:, begin : begin + PIXELS * PACK],
                 )
 
-        def add_position(total, a, k, pair):
+        def add_positions(total, a, pair, ks, start, stop):
             cols = slice((a % 2) * P, (a % 2 + 1) * P)
-            nc.tensor.matmul_mx(
-                out=total[:],
-                lhsT=w1_codes[:, a // 2, k, cols].bitcast(FP8X4),
-                lhsT_scale=w1_scales[:, a // 2, k, cols],
-                rhs=h_codes[:, k, pair, :].bitcast(FP8X4),
-                rhs_scale=h_scales[:, k, pair, :],
-                start=(k == 0),
-                stop=(k == CENTRE - 1),
-            )
-
-        centre = keep.tile([P, TILES, PIXELS], F32)
-
-        def centre_product():
-            for pair in range(TILES // 2):
-                product = bank([P, 2, PIXELS])
-                for half in range(2):
-                    cols = slice(half * P, (half + 1) * P)
-                    nc.tensor.matmul_mx(
-                        out=product[:, half, :],
-                        lhsT=w1_codes[:, pair, CENTRE, cols].bitcast(FP8X4),
-                        lhsT_scale=w1_scales[:, pair, CENTRE, cols],
-                        rhs=h_codes[:, CENTRE, 0, 0:PIXELS].bitcast(FP8X4),
-                        rhs_scale=h_scales[:, CENTRE, 0, 0:PIXELS],
-                        start=True,
-                        stop=True,
-                    )
-                nc.scalar.copy(out=centre[:, 2 * pair : 2 * pair + 2, :], in_=product[:])
+            for i, k in enumerate(ks):
+                source = 0 if k == CENTRE else pair
+                nc.tensor.matmul_mx(
+                    out=total[:],
+                    lhsT=w1_codes[:, a // 2, k, cols].bitcast(FP8X4),
+                    lhsT_scale=w1_scales[:, a // 2, k, cols],
+                    rhs=h_codes[:, k, source, :].bitcast(FP8X4),
+                    rhs_scale=h_scales[:, k, source, :],
+                    start=start and i == 0,
+                    stop=stop and i == len(ks) - 1,
+                )
 
         out_dram = out[0].rearrange("(a q) (s r) h w -> a s q (r h w)", q=P, s=2)
 
-        def store(total, a, pair):
-            result = stage.tile([P, 2 * PIXELS], F32, name="result")
-            nc.vector.tensor_tensor(
-                out=result[:].rearrange("q (r n) -> q r n", r=2),
-                in0=total[:].rearrange("q (r n) -> q r n", r=2),
-                in1=centre[:, a, :].unsqueeze(1).to_broadcast([P, 2, PIXELS]),
-                op=mybir.AluOpType.add,
-            )
-            nc.sync.dma_start(out=out_dram[a, pair], in_=result[:])
-
-        groups = [(a, pair) for pair in range(ROTATIONS // 2) for a in range(TILES)]
-        totals = [bank([P, 2 * PIXELS]) for g in range(EARLY_GROUPS)]
-        for k in range(WEIGHTS_LEAD):
-            weights(k)
-        for k in range(HIDDEN_LEAD):
-            hidden_layer(k)
-        for k in range(NUM_K):
-            if k + WEIGHTS_LEAD < NUM_K:
-                weights(k + WEIGHTS_LEAD)
-            if k + HIDDEN_LEAD < NUM_K:
-                hidden_layer(k + HIDDEN_LEAD)
-            if k == CENTRE:
-                centre_product()
-            else:
-                for g in range(EARLY_GROUPS):
-                    add_position(totals[g], groups[g][0], k, groups[g][1])
-        for g in range(EARLY_GROUPS):
-            store(totals[g], groups[g][0], groups[g][1])
-        for g in range(EARLY_GROUPS, len(groups)):
-            total = bank([P, 2 * PIXELS])
-            for k in range(CENTRE):
-                add_position(total, groups[g][0], k, groups[g][1])
-            store(total, groups[g][0], groups[g][1])
+        with tc.manual_schedule():
+            prepare_x()
+            for t in (0, 1):
+                for g in range(NUM_K // PLANES):
+                    take_apart(t, g)
+            for g, copies in enumerate([[(2, 0)], [(2, 1), (3, 0)], []]):
+                for k in ORDER[g * PLANES : (g + 1) * PLANES]:
+                    prepare("w", k, 0)
+                for t, planes_of in copies:
+                    take_apart(t, planes_of)
+            totals = [bank([P, 2 * PIXELS]) for a in range(TILES)]
+            parts = []
+            for p in range(-WEIGHTS_LEAD, NUM_K):
+                if p >= 0:
+                    k = ORDER[p]
+                    quantise_all("w1", k)
+                    for a in range(TILES):
+                        add_positions(totals[a], a, 0, [k], p == 0, p == NUM_K - 1)
+                    if p >= FIRST_PART - 1 and len(parts) < TILES:
+                        a = len(parts)
+                        total = bank([P, 2 * PIXELS])
+                        add_positions(total, a, 1, ORDER[:FIRST_PART], True, True)
+                        part = keep.tile([P, 2 * PIXELS], F32, name="part%d" % a)
+                        nc.scalar.copy(out=part[:], in_=total[:])
+                        parts.append(part)
+                if p + WEIGHTS_LEAD < NUM_K:
+                    prepare("w", ORDER[p + WEIGHTS_LEAD], 1)
+                    for pair in range(TILES // 2):
+                        prepare("w1", ORDER[p + WEIGHTS_LEAD], pair)
+                if 0 <= p + H_LEAD < NUM_K:
+                    quantise_h(ORDER[p + H_LEAD])
+                if 0 <= p + STEP_1_LEAD < NUM_K:
+                    quantise_all("w", ORDER[p + STEP_1_LEAD])
+                    step_1(ORDER[p + STEP_1_LEAD])
+                if p == -WEIGHTS_LEAD:
+                    take_apart(2, 2)
+                    take_apart(3, 1)
+                if p == 1 - WEIGHTS_LEAD:
+                    take_apart(3, 2)
+            for a in range(TILES):
+                result = results.tile([P, 2 * PIXELS], F32, name="result")
+                nc.scalar.copy(out=result[:], in_=totals[a][:])
+                nc.sync.dma_start(out=out_dram[a, 0], in_=result[:])
+            for a in range(TILES):
+                total = bank([P, 2 * PIXELS])
+                add_positions(total, a, 1, ORDER[FIRST_PART:], True, True)
+                result = results.tile([P, 2 * PIXELS], F32, name="result")
+                nc.vector.tensor_tensor(out=result[:], in0=total[:], in1=parts[a][:], op=ADD)
+                nc.sync.dma_start(out=out_dram[a, 1], in_=result[:])

@@ -50,16 +50,6 @@ def tile_psr4convf_kernel(tc, x, W, W1, out):
         def bank(shape):
             return psum.tile(shape, F32, tag="bank", name="bank")
 
-        ident = keep.tile([P, P], F32)
-        masks.make_identity(nc, ident[:])
-        padded = (SIDE + 2) * SIDE * PACK
-        h_image = {}
-        for dx in (-1, 0, 1):
-            for slot in range(2):
-                image = keep.tile([P, padded], BF16, align_bytes=64, name="h_image_%d_%d" % (dx + 1, slot))
-                nc.gpsimd.memset(image[:].bitcast(F32), 0.0)
-                h_image[(dx, slot)] = image
-
         x_rows = keep.tile([P, PACK, PIXELS], BF16)
         nc.sync.dma_start(out=x_rows[:], in_=x[0].rearrange("(q t) h w -> q t (h w)", t=PACK))
         w_dram = W.rearrange("(q t) c k -> t q (c k)", t=PACK)
@@ -74,6 +64,16 @@ def tile_psr4convf_kernel(tc, x, W, W1, out):
             rows = w1_in.tile([P, TILES * CH], BF16, name="w1_rows")
             nc.sync.dma_start(out=rows[:].rearrange("q (a o) -> q a o", a=TILES), in_=w1_dram[k])
             w1_rows[k] = rows
+
+        ident = keep.tile([P, P], F32)
+        masks.make_identity(nc, ident[:])
+        padded = (SIDE + 2) * SIDE * PACK
+        h_image = {}
+        for dx in (-1, 0, 1):
+            for slot in range(2):
+                image = keep.tile([P, padded], BF16, align_bytes=64, name="h_image_%d_%d" % (dx + 1, slot))
+                nc.gpsimd.memset(image[:].bitcast(F32), 0.0)
+                h_image[(dx, slot)] = image
 
         x_grouped = keep.tile([P, PIXELS, PACK], BF16, align_bytes=64)
         x_codes = keep.tile([P, PIXELS], U32, align_bytes=64)
@@ -171,18 +171,21 @@ def tile_psr4convf_kernel(tc, x, W, W1, out):
                     func=RELU,
                 )
 
+        def shift_columns(k):
+            if k == CENTRE:
+                return
+            slot = ORDER.index(k) % 2
+            src = h_image[(0, slot)][:].rearrange("q (i j t) -> q i j t", j=SIDE, t=PACK)
+            for dx in (-1, 1):
+                lo, hi = max(0, -dx), SIDE - max(0, dx)
+                dst = h_image[(dx, slot)][:].rearrange("q (i j t) -> q i j t", j=SIDE, t=PACK)
+                nc.vector.tensor_copy(
+                    out=dst[:, 1 : SIDE + 1, lo:hi, :], in_=src[:, 1 : SIDE + 1, lo + dx : hi + dx, :]
+                )
+
         def quantise_h(k):
             slot = ORDER.index(k) % 2
-            centred = h_image[(0, slot)]
             shifts = [shift_of(k, r) for r in range(2 if k == CENTRE else ROTATIONS)]
-            for dx in (-1, 1):
-                if any(s[1] == dx for s in shifts):
-                    lo, hi = max(0, -dx), SIDE - max(0, dx)
-                    src = centred[:].rearrange("q (i j t) -> q i j t", j=SIDE, t=PACK)
-                    dst = h_image[(dx, slot)][:].rearrange("q (i j t) -> q i j t", j=SIDE, t=PACK)
-                    nc.vector.tensor_copy(
-                        out=dst[:, 1 : SIDE + 1, lo:hi, :], in_=src[:, 1 : SIDE + 1, lo + dx : hi + dx, :]
-                    )
             for r, (dy, dx) in enumerate(shifts):
                 begin = (1 + dy) * SIDE * PACK
                 cols = slice((r % 2) * PIXELS, (r % 2 + 1) * PIXELS)
@@ -192,7 +195,7 @@ def tile_psr4convf_kernel(tc, x, W, W1, out):
                     in_=h_image[(dx, slot)][:, begin : begin + PIXELS * PACK],
                 )
 
-        def add_positions(total, a, pair, ks, start, stop):
+        def add_positions(total, a, pair, ks, start, stop, pixels=slice(0, 2 * PIXELS)):
             cols = slice((a % 2) * P, (a % 2 + 1) * P)
             for i, k in enumerate(ks):
                 source = 0 if k == CENTRE else pair
@@ -200,8 +203,8 @@ def tile_psr4convf_kernel(tc, x, W, W1, out):
                     out=total[:],
                     lhsT=w1_codes[:, a // 2, k, cols].bitcast(FP8X4),
                     lhsT_scale=w1_scales[:, a // 2, k, cols],
-                    rhs=h_codes[:, k, source, :].bitcast(FP8X4),
-                    rhs_scale=h_scales[:, k, source, :],
+                    rhs=h_codes[:, k, source, pixels].bitcast(FP8X4),
+                    rhs_scale=h_scales[:, k, source, pixels],
                     start=start and i == 0,
                     stop=stop and i == len(ks) - 1,
                 )
@@ -213,13 +216,14 @@ def tile_psr4convf_kernel(tc, x, W, W1, out):
             for t in (0, 1):
                 for g in range(NUM_K // PLANES):
                     take_apart(t, g)
-            for g, copies in enumerate([[(2, 0)], [(2, 1), (3, 0)], []]):
+            for g, copies in enumerate([[(2, 0), (3, 0)], [], []]):
                 for k in ORDER[g * PLANES : (g + 1) * PLANES]:
                     prepare("w", k, 0)
                 for t, planes_of in copies:
                     take_apart(t, planes_of)
             totals = [bank([P, 2 * PIXELS]) for a in range(TILES)]
             parts = []
+            late_copies = [(2, 1), (3, 1), (2, 2), (3, 2)]
             for p in range(-WEIGHTS_LEAD, NUM_K):
                 if p >= 0:
                     k = ORDER[p]
@@ -235,6 +239,9 @@ def tile_psr4convf_kernel(tc, x, W, W1, out):
                         parts.append(part)
                 if p + WEIGHTS_LEAD < NUM_K:
                     prepare("w", ORDER[p + WEIGHTS_LEAD], 1)
+                if 0 <= p + H_LEAD < NUM_K:
+                    shift_columns(ORDER[p + H_LEAD])
+                if p + WEIGHTS_LEAD < NUM_K:
                     for pair in range(TILES // 2):
                         prepare("w1", ORDER[p + WEIGHTS_LEAD], pair)
                 if 0 <= p + H_LEAD < NUM_K:
@@ -242,18 +249,18 @@ def tile_psr4convf_kernel(tc, x, W, W1, out):
                 if 0 <= p + STEP_1_LEAD < NUM_K:
                     quantise_all("w", ORDER[p + STEP_1_LEAD])
                     step_1(ORDER[p + STEP_1_LEAD])
-                if p == -WEIGHTS_LEAD:
-                    take_apart(2, 2)
-                    take_apart(3, 1)
-                if p == 1 - WEIGHTS_LEAD:
-                    take_apart(3, 2)
+                if late_copies:
+                    take_apart(*late_copies.pop(0))
             for a in range(TILES):
                 result = results.tile([P, 2 * PIXELS], F32, name="result")
                 nc.scalar.copy(out=result[:], in_=totals[a][:])
                 nc.sync.dma_start(out=out_dram[a, 0], in_=result[:])
             for a in range(TILES):
-                total = bank([P, 2 * PIXELS])
-                add_positions(total, a, 1, ORDER[FIRST_PART:], True, True)
-                result = results.tile([P, 2 * PIXELS], F32, name="result")
-                nc.vector.tensor_tensor(out=result[:], in0=total[:], in1=parts[a][:], op=ADD)
-                nc.sync.dma_start(out=out_dram[a, 1], in_=result[:])
+                width = PIXELS if a == TILES - 1 else 2 * PIXELS
+                for begin in range(0, 2 * PIXELS, width):
+                    pixels = slice(begin, begin + width)
+                    total = bank([P, width])
+                    add_positions(total, a, 1, ORDER[FIRST_PART:], True, True, pixels)
+                    result = results.tile([P, width], F32, name="result")
+                    nc.vector.tensor_tensor(out=result[:], in0=total[:], in1=parts[a][:, pixels], op=ADD)
+                    nc.sync.dma_start(out=out_dram[a, 1][:, pixels], in_=result[:])

@@ -200,7 +200,7 @@ def tile_psr4convf_kernel(tc, x, W, W1, out):
             for i, k in enumerate(ks):
                 source = 0 if k == CENTRE else pair
                 nc.tensor.matmul_mx(
-                    out=total[:],
+                    out=total,
                     lhsT=w1_codes[:, a // 2, k, cols].bitcast(FP8X4),
                     lhsT_scale=w1_scales[:, a // 2, k, cols],
                     rhs=h_codes[:, k, source, pixels].bitcast(FP8X4),
@@ -208,6 +208,20 @@ def tile_psr4convf_kernel(tc, x, W, W1, out):
                     start=start and i == 0,
                     stop=stop and i == len(ks) - 1,
                 )
+
+        centre = keep.tile([P, TILES, PIXELS], F32)
+
+        def multiply_centre():
+            for pair in range(TILES // 2):
+                product = bank([P, 2, PIXELS])
+                for half in range(2):
+                    add_positions(product[:, half, :], 2 * pair + half, 0, [CENTRE], True, True, slice(0, PIXELS))
+                nc.scalar.copy(out=centre[:, 2 * pair : 2 * pair + 2, :], in_=product[:])
+
+        def add_centre(part, a):
+            twice = centre[:, a : a + 1, :].to_broadcast([P, 2, PIXELS])
+            sums = part[:].rearrange("q (r n) -> q r n", r=2)
+            nc.vector.tensor_tensor(out=sums, in0=sums, in1=twice, op=ADD)
 
         out_dram = out[0].rearrange("(a q) (s r) h w -> a s q (r h w)", q=P, s=2)
 
@@ -228,12 +242,14 @@ def tile_psr4convf_kernel(tc, x, W, W1, out):
                 if p >= 0:
                     k = ORDER[p]
                     quantise_all("w1", k)
+                    if p == NUM_K - 2:
+                        multiply_centre()
                     for a in range(TILES):
-                        add_positions(totals[a], a, 0, [k], p == 0, p == NUM_K - 1)
+                        add_positions(totals[a][:], a, 0, [k], p == 0, p == NUM_K - 1)
                     if p >= FIRST_PART - 1 and len(parts) < TILES:
                         a = len(parts)
                         total = bank([P, 2 * PIXELS])
-                        add_positions(total, a, 1, ORDER[:FIRST_PART], True, True)
+                        add_positions(total[:], a, 1, ORDER[1:FIRST_PART], True, True)
                         part = keep.tile([P, 2 * PIXELS], F32, name="part%d" % a)
                         nc.scalar.copy(out=part[:], in_=total[:])
                         parts.append(part)
@@ -252,6 +268,8 @@ def tile_psr4convf_kernel(tc, x, W, W1, out):
                 if late_copies:
                     take_apart(*late_copies.pop(0))
             for a in range(TILES):
+                add_centre(parts[a], a)
+            for a in range(TILES):
                 result = results.tile([P, 2 * PIXELS], F32, name="result")
                 nc.scalar.copy(out=result[:], in_=totals[a][:])
                 nc.sync.dma_start(out=out_dram[a, 0], in_=result[:])
@@ -260,7 +278,7 @@ def tile_psr4convf_kernel(tc, x, W, W1, out):
                 for begin in range(0, 2 * PIXELS, width):
                     pixels = slice(begin, begin + width)
                     total = bank([P, width])
-                    add_positions(total, a, 1, ORDER[FIRST_PART:], True, True, pixels)
+                    add_positions(total[:], a, 1, ORDER[FIRST_PART:], True, True, pixels)
                     result = results.tile([P, width], F32, name="result")
                     nc.vector.tensor_tensor(out=result[:], in0=total[:], in1=parts[a][:, pixels], op=ADD)
                     nc.sync.dma_start(out=out_dram[a, 1][:, pixels], in_=result[:])

@@ -218,10 +218,10 @@ def tile_psr4convf_kernel(tc, x, W, W1, out):
                     add_positions(product[:, half, :], 2 * pair + half, 0, [CENTRE], True, True, slice(0, PIXELS))
                 nc.scalar.copy(out=centre[:, 2 * pair : 2 * pair + 2, :], in_=product[:])
 
-        def add_centre(part, a):
+        def add_centre(into, sums, a):
             twice = centre[:, a : a + 1, :].to_broadcast([P, 2, PIXELS])
-            sums = part[:].rearrange("q (r n) -> q r n", r=2)
-            nc.vector.tensor_tensor(out=sums, in0=sums, in1=twice, op=ADD)
+            into, sums = (t[:].rearrange("q (r n) -> q r n", r=2) for t in (into, sums))
+            nc.vector.tensor_tensor(out=into, in0=sums, in1=twice, op=ADD)
 
         out_dram = out[0].rearrange("(a q) (s r) h w -> a s q (r h w)", q=P, s=2)
 
@@ -244,8 +244,9 @@ def tile_psr4convf_kernel(tc, x, W, W1, out):
                     quantise_all("w1", k)
                     if p == NUM_K - 2:
                         multiply_centre()
-                    for a in range(TILES):
-                        add_positions(totals[a][:], a, 0, [k], p == 0, p == NUM_K - 1)
+                    for a in range(TILES if p > 0 else TILES - 1):
+                        first = 1 if a == TILES - 1 else 0
+                        add_positions(totals[a][:], a, 0, [k], p == first, p == NUM_K - 1)
                     if p >= FIRST_PART - 1 and len(parts) < TILES:
                         a = len(parts)
                         total = bank([P, 2 * PIXELS])
@@ -268,10 +269,13 @@ def tile_psr4convf_kernel(tc, x, W, W1, out):
                 if late_copies:
                     take_apart(*late_copies.pop(0))
             for a in range(TILES):
-                add_centre(parts[a], a)
+                add_centre(parts[a], parts[a], a)
             for a in range(TILES):
                 result = results.tile([P, 2 * PIXELS], F32, name="result")
-                nc.scalar.copy(out=result[:], in_=totals[a][:])
+                if a < TILES - 1:
+                    nc.scalar.copy(out=result[:], in_=totals[a][:])
+                else:
+                    add_centre(result, totals[a], a)
                 nc.sync.dma_start(out=out_dram[a, 0], in_=result[:])
             for a in range(TILES):
                 width = PIXELS if a == TILES - 1 else 2 * PIXELS

from contextlib import ExitStack

import concourse.masks as masks
import concourse.mybir as mybir

BF16 = mybir.dt.bfloat16
F32 = mybir.dt.float32
U32 = mybir.dt.uint32
U8 = mybir.dt.uint8
FP8X4 = mybir.dt.float8_e4m3fn_x4
RELU = mybir.ActivationFunctionType.Relu
ADD = mybir.AluOpType.add

P = 128
PACK = 4
CH = 512
TILES = CH // P
NUM_K = 9
CENTRE = 8
SIDE = 16
PIXELS = SIDE * SIDE
ROTATIONS = 4
RING = [(-1, -1), (-1, 0), (-1, 1), (0, 1), (1, 1), (1, 0), (1, -1), (0, -1)]
PLANES = 3
BANKS = 8
ORDER = [8, 6, 7, 0, 1, 2, 3, 4, 5]
FIRST_PART = 5
BEHIND = 2
WEIGHTS_LEAD = 4
STEP_1_LEAD = 3
H_LEAD = 2

FLOPS = 2 * 2 * NUM_K * CH * CH * PIXELS


def shift_of(k, r):
    return (0, 0) if k == CENTRE else RING[(k + 2 * r) % len(RING)]


def tile_psr4convf_kernel(tc, x, W, W1, out):
    nc = tc.nc
    with ExitStack() as ctx:
        keep = ctx.enter_context(tc.tile_pool(name="keep", bufs=1))
        w_in = ctx.enter_context(tc.tile_pool(name="w_in", bufs=3))
        w1_in = ctx.enter_context(tc.tile_pool(name="w1_in", bufs=5))
        stage = ctx.enter_context(tc.tile_pool(name="stage", bufs=8))
        results = ctx.enter_context(tc.tile_pool(name="results", bufs=6))
        psum = ctx.enter_context(tc.psum_pool(name="psum", bufs=BANKS))

        def bank(shape):
            return psum.tile(shape, F32, tag="bank", name="bank")

        x_rows = keep.tile([P, PACK, PIXELS], BF16)
        nc.sync.dma_start(out=x_rows[:], in_=x[0].rearrange("(q t) h w -> q t (h w)", t=PACK))
        w_dram = W.rearrange("(q t) c k -> t q (c k)", t=PACK)
        w_rows = []
        for t in range(TILES):
            rows = w_in.tile([P, CH * NUM_K], BF16, name="w_rows")
            nc.sync.dma_start(out=rows[:], in_=w_dram[t])
            w_rows.append(rows)
        w1_dram = W1.rearrange("(a q) (k o) -> k q a o", q=P, k=NUM_K)
        w1_rows = {}
        for k in ORDER:
            rows = w1_in.tile([P, TILES * CH], BF16, name="w1_rows")
            nc.sync.dma_start(out=rows[:].rearrange("q (a o) -> q a o", a=TILES), in_=w1_dram[k])
            w1_rows[k] = rows

        ident = keep.tile([P, P], F32)
        masks.make_identity(nc, ident[:])
        padded = (SIDE + 2) * SIDE * PACK
        h_image = {}
        for dx in (-1, 0, 1):
            for slot in range(2):
                image = keep.tile([P, padded], BF16, align_bytes=64, name="h_image_%d_%d" % (dx + 1, slot))
                nc.gpsimd.memset(image[:].bitcast(F32), 0.0)
                h_image[(dx, slot)] = image

        x_grouped = keep.tile([P, PIXELS, PACK], BF16, align_bytes=64)
        x_codes = keep.tile([P, PIXELS], U32, align_bytes=64)
        x_scales = keep.tile([P, PIXELS], U8, align_bytes=64)

        def prepare_x():
            nc.vector.tensor_copy(out=x_grouped[:], in_=x_rows[:].rearrange("q t n -> q n t"))
            nc.vector.quantize_mx(
                out=x_codes[:].bitcast(FP8X4),
                scales=x_scales[:],
                in_=x_grouped[:].rearrange("q n t -> q (n t)"),
            )

        def transpose(blocks):
            n = len(blocks)
            turned = bank([P, n, 2, P])
            for b, halves in enumerate(blocks):
                for u in range(2):
                    nc.tensor.transpose(turned[:, b, u, :], halves[u], ident[:])
            grouped = stage.tile([P, n * P * PACK], BF16, align_bytes=64, name="grouped")
            nc.scalar.copy(
                out=grouped[:].bitcast(F32).rearrange("q (b c u) -> q b c u", b=n, u=2),
                in_=turned[:].rearrange("q b u c -> q b c u"),
            )
            return grouped

        w_by_k = [keep.tile([P, NUM_K * CH], BF16, name="w_by_k%d" % t) for t in range(TILES)]

        def take_apart(t, g):
            first = min(ORDER[g * PLANES : (g + 1) * PLANES])
            ks = slice(first, first + PLANES)
            src = w_rows[t][:].rearrange("p (q u e k) -> p u q e k", u=2, e=2, k=NUM_K)[:, :, :, :, ks]
            dst = w_by_k[t][:].rearrange("p (k u q e) -> p u q e k", u=2, e=2, k=NUM_K)[:, :, :, :, ks]
            if t == 0 and g == 2:
                for u in range(2):
                    nc.scalar.copy(out=dst[:, u], in_=src[:, u])
            else:
                nc.vector.tensor_copy(out=dst, in_=src)

        w_codes = keep.tile([P, TILES // 2, NUM_K, 2 * P], U32, align_bytes=64)
        w_scales = keep.tile([P, TILES // 2, NUM_K, 2 * P], U8, align_bytes=64)
        w1_codes = keep.tile([P, TILES // 2, NUM_K, 2 * P], U32, align_bytes=64)
        w1_scales = keep.tile([P, TILES // 2, NUM_K, 2 * P], U8, align_bytes=64)

        pending = []

        def quantise(unit):
            which, k, pair, grouped = unit
            codes, scales = (w_codes, w_scales) if which == "w" else (w1_codes, w1_scales)
            nc.vector.quantize_mx(
                out=codes[:, pair, k, :].bitcast(FP8X4), scales=scales[:, pair, k, :], in_=grouped[:]
            )

        def quantise_all(which, k):
            for unit in list(pending):
                if unit[0] == which and unit[1] == k:
                    quantise(unit)
                    pending.remove(unit)

        def prepare(which, k, pair):
            tiles = (2 * pair, 2 * pair + 1)
            if which == "w":
                words = [w_by_k[t][:].bitcast(F32).rearrange("p (k u q) -> p k u q", k=NUM_K, u=2)[:, k] for t in tiles]
            else:
                rows = w1_rows[k][:].bitcast(F32).rearrange("p (a q u) -> p a u q", a=TILES, u=2)
                words = [rows[:, a] for a in tiles]
            pending.append((which, k, pair, transpose([[w[:, u, :] for u in range(2)] for w in words])))
            while len(pending) > BEHIND:
                quantise(pending.pop(0))

        h_codes = keep.tile([P, NUM_K, ROTATIONS // 2, 2 * PIXELS], U32, align_bytes=64)
        h_scales = keep.tile([P, NUM_K, ROTATIONS // 2, 2 * PIXELS], U8, align_bytes=64)

        def step_1(k):
            centred = h_image[(0, ORDER.index(k) % 2)]
            half_pixels = PIXELS // 2
            for half in range(2):
                z = bank([P, PACK, half_pixels])
                pixels = slice(half * half_pixels, (half + 1) * half_pixels)
                for t in range(TILES):
                    cols = slice((t % 2) * P, (t % 2 + 1) * P)
                    nc.tensor.matmul_mx(
                        out=z[:, t, :],
                        lhsT=w_codes[:, t // 2, k, cols].bitcast(FP8X4),
                        lhsT_scale=w_scales[:, t // 2, k, cols],
                        rhs=x_codes[:, pixels].bitcast(FP8X4),
                        rhs_scale=x_scales[:, pixels],
                        start=True,
                        stop=True,
                    )
                begin = (SIDE + half * half_pixels) * PACK
                nc.scalar.activation(
                    out=centred[:, begin : begin + half_pixels * PACK].rearrange("q (n t) -> q n t", t=PACK),
                    in_=z[:].rearrange("q t n -> q n t"),
                    func=RELU,
                )

        def shift_columns(k):
            if k == CENTRE:
                return
            slot = ORDER.index(k) % 2
            src = h_image[(0, slot)][:].rearrange("q (i j t) -> q i j t", j=SIDE, t=PACK)
            for dx in (-1, 1):
                lo, hi = max(0, -dx), SIDE - max(0, dx)
                dst = h_image[(dx, slot)][:].rearrange("q (i j t) -> q i j t", j=SIDE, t=PACK)
                nc.vector.tensor_copy(
                    out=dst[:, 1 : SIDE + 1, lo:hi, :], in_=src[:, 1 : SIDE + 1, lo + dx : hi + dx, :]
                )

        def quantise_h(k):
            slot = ORDER.index(k) % 2
            shifts = [shift_of(k, r) for r in range(2 if k == CENTRE else ROTATIONS)]
            for r, (dy, dx) in enumerate(shifts):
                begin = (1 + dy) * SIDE * PACK
                cols = slice((r % 2) * PIXELS, (r % 2 + 1) * PIXELS)
                nc.vector.quantize_mx(
                    out=h_codes[:, k, r // 2, cols].bitcast(FP8X4),
                    scales=h_scales[:, k, r // 2, cols],
                    in_=h_image[(dx, slot)][:, begin : begin + PIXELS * PACK],
                )

        def add_positions(total, a, pair, ks, start, stop, pixels=slice(0, 2 * PIXELS)):
            cols = slice((a % 2) * P, (a % 2 + 1) * P)
            for i, k in enumerate(ks):
                source = 0 if k == CENTRE else pair
                nc.tensor.matmul_mx(
                    out=total,
                    lhsT=w1_codes[:, a // 2, k, cols].bitcast(FP8X4),
                    lhsT_scale=w1_scales[:, a // 2, k, cols],
                    rhs=h_codes[:, k, source, pixels].bitcast(FP8X4),
                    rhs_scale=h_scales[:, k, source, pixels],
                    start=start and i == 0,
                    stop=stop and i == len(ks) - 1,
                )

        centre = keep.tile([P, TILES, PIXELS], F32)

        def multiply_centre():
            for pair in range(TILES // 2):
                product = bank([P, 2, PIXELS])
                for half in range(2):
                    add_positions(product[:, half, :], 2 * pair + half, 0, [CENTRE], True, True, slice(0, PIXELS))
                nc.scalar.copy(out=centre[:, 2 * pair : 2 * pair + 2, :], in_=product[:])

        def add_centre(into, sums, a):
            twice = centre[:, a : a + 1, :].to_broadcast([P, 2, PIXELS])
            into, sums = (t[:].rearrange("q (r n) -> q r n", r=2) for t in (into, sums))
            nc.vector.tensor_tensor(out=into, in0=sums, in1=twice, op=ADD)

        out_dram = out[0].rearrange("(a q) (s r) h w -> a s q (r h w)", q=P, s=2)

        with tc.manual_schedule():
            prepare_x()
            for t in (0, 1):
                for g in range(NUM_K // PLANES):
                    take_apart(t, g)
            for g, copies in enumerate([[(2, 0), (3, 0)], [], []]):
                for k in ORDER[g * PLANES : (g + 1) * PLANES]:
                    prepare("w", k, 0)
                for t, planes_of in copies:
                    take_apart(t, planes_of)
            totals = [bank([P, 2 * PIXELS]) for a in range(TILES)]
            parts = []
            late_copies = [(2, 1), (3, 1), (2, 2), (3, 2)]
            for p in range(-WEIGHTS_LEAD, NUM_K):
                if p >= 0:
                    k = ORDER[p]
                    quantise_all("w1", k)
                    if p == NUM_K - 2:
                        multiply_centre()
                    for a in range(TILES if p > 0 else TILES - 1):
                        first = 1 if a == TILES - 1 else 0
                        add_positions(totals[a][:], a, 0, [k], p == first, p == NUM_K - 1)
                    if p >= FIRST_PART - 1 and len(parts) < TILES:
                        a = len(parts)
                        total = bank([P, 2 * PIXELS])
                        add_positions(total[:], a, 1, ORDER[1:FIRST_PART], True, True)
                        part = keep.tile([P, 2 * PIXELS], F32, name="part%d" % a)
                        nc.scalar.copy(out=part[:], in_=total[:])
                        parts.append(part)
                if p + WEIGHTS_LEAD < NUM_K:
                    prepare("w", ORDER[p + WEIGHTS_LEAD], 1)
                if 0 <= p + H_LEAD < NUM_K:
                    shift_columns(ORDER[p + H_LEAD])
                if p + WEIGHTS_LEAD < NUM_K:
                    for pair in range(TILES // 2):
                        prepare("w1", ORDER[p + WEIGHTS_LEAD], pair)
                if 0 <= p + H_LEAD < NUM_K:
                    quantise_h(ORDER[p + H_LEAD])
                if 0 <= p + STEP_1_LEAD < NUM_K:
                    quantise_all("w", ORDER[p + STEP_1_LEAD])
                    step_1(ORDER[p + STEP_1_LEAD])
                if late_copies:
                    take_apart(*late_copies.pop(0))
            for a in range(TILES):
                add_centre(parts[a], parts[a], a)
            for a in range(TILES):
                result = results.tile([P, 2 * PIXELS], F32, name="result")
                if a < TILES - 1:
                    nc.scalar.copy(out=result[:], in_=totals[a][:])
                else:
                    add_centre(result, totals[a], a)
                nc.sync.dma_start(out=out_dram[a, 0], in_=result[:])
            for a in range(TILES):
                width = PIXELS if a == TILES - 1 else 2 * PIXELS
                for begin in range(0, 2 * PIXELS, width):
                    pixels = slice(begin, begin + width)
                    total = bank([P, width])
                    add_positions(total[:], a, 1, ORDER[FIRST_PART:], True, True, pixels)
                    result = results.tile([P, width], F32, name="result")
                    nc.vector.tensor_tensor(out=result[:], in0=total[:], in1=parts[a][:, pixels], op=ADD)
                    nc.sync.dma_start(out=out_dram[a, 1][:, pixels], in_=result[:])
